import numpy as np
import ml_dtypes


def mxq(x, axis, fmt="e4m3"):
    dtype, down = {"e4m3": (ml_dtypes.float8_e4m3fn, 7), "e5m2": (ml_dtypes.float8_e5m2, 14)}[fmt]
    v = np.moveaxis(np.asarray(x, np.float32).astype(ml_dtypes.bfloat16).astype(np.float64), axis, -1)
    blocks = v.reshape(v.shape[:-1] + (-1, 32))
    amax = np.abs(blocks).max(-1, keepdims=True)
    byte = np.maximum(np.where(amax > 0, np.frexp(amax)[1] - 1 + 127, 0) - down, 1)
    scale = np.exp2(byte - 127.0)
    codes = (blocks / scale).astype(np.float32).astype(dtype).astype(np.float64)
    return np.moveaxis((codes * scale).reshape(v.shape), -1, axis)


WIDE = False


def mx_kscale(k):
    if not WIDE:
        return np.ones(k)
    levels = np.array([10, -10, 5, -5, 0])
    a = np.random.permutation(np.resize(levels, k // 512 * 4)).reshape(k // 512, 4)
    idx = np.arange(k)
    return np.exp2(a[idx // 512, idx % 128 // 32])


BF16 = ml_dtypes.bfloat16


def bf(x):
    return np.asarray(x, np.float32).astype(BF16)


def f64(x):
    return np.asarray(x).astype(np.float64)


B, S, H, E, D, TRAIN_LEN = 1, 1024, 1024, 1536, 128, 512


def silu(v):
    return v / (1.0 + np.exp(-v))


def apply_rotary(x, sin, cos):
    x1, x2 = x[..., 0::2], x[..., 1::2]
    return np.concatenate([x1 * cos - x2 * sin, x1 * sin + x2 * cos], axis=-1)


def setup_inputs():
    s = mx_kscale(H)
    pos = np.arange(S)[:, None]
    inv = np.exp(-np.arange(0, D, 2) / D * np.log(10000.0))
    ang = pos * inv[None, :]
    return {"hidden_states": bf(np.random.standard_normal((B, S, H)) * s),
            "sin": bf(np.sin(ang)[None]),
            "cos": bf(np.cos(ang)[None]),
            "W_i": bf(np.random.standard_normal((H, 2 * E + D)) / np.sqrt(H) / s[:, None]),
            "q_scale": bf(1.0 + 0.1 * np.random.standard_normal(D)),
            "k_scale": bf(1.0 + 0.1 * np.random.standard_normal(D))}


def reference(hidden_states, sin, cos, W_i, q_scale, k_scale):
    x = silu(mxq(f64(hidden_states), 2, "e4m3") @ mxq(f64(W_i), 0, "e4m3"))
    u, v, qk = np.split(x, [E, 2 * E], axis=-1)
    sn, cs = f64(sin), f64(cos)
    q = apply_rotary(qk * f64(q_scale), sn, cs)
    k = apply_rotary(qk * f64(k_scale), sn, cs)
    return u, v, q, k

@@ -1,0 +1,237 @@
+from contextlib import ExitStack
+
+import concourse.mybir as mybir
+from concourse.masks import make_identity
+
+F32 = mybir.dt.float32
+BF16 = mybir.dt.bfloat16
+U32 = mybir.dt.uint32
+U8 = mybir.dt.uint8
+FP8X4 = mybir.dt.float8_e4m3fn_x4
+SILU = mybir.ActivationFunctionType.Silu
+MULT = mybir.AluOpType.mult
+ADD = mybir.AluOpType.add
+SUB = mybir.AluOpType.subtract
+
+P = 128
+NT = 8
+E = 1536
+D = 128
+CH = 512
+VW = E + D
+
+FLOPS = 2 * 1024 * 1024 * 3200
+
+
+def tile_gatedattentionunit_pa_kernel(
+    tc, hidden_states, sin, cos, W_i, q_scale, k_scale, out_0, out_1, out_2, out_3
+):
+    nc = tc.nc
+    x_dram = hidden_states.flatten_outer_dims().rearrange("(p i) k -> p i k", i=NT)
+    cos_dram = cos.flatten_outer_dims().rearrange("(p i) j -> p i j", i=NT)
+    sin_dram = sin.flatten_outer_dims().rearrange("(p i) j -> p i j", i=NT)
+    w_by_e = W_i.rearrange("(a q e) n -> e q a n", a=4, e=2)
+    w_by_a = W_i.rearrange("(a q e) n -> a q e n", a=4, e=2)
+    u_dram = out_0.flatten_outer_dims().rearrange("(p i) c -> i p c", i=NT)
+    v_dram = out_1.flatten_outer_dims().rearrange("(p i) c -> i p c", i=NT)
+    q_dram = out_2.flatten_outer_dims().rearrange("(p i) c -> p i c", i=NT)
+    k_dram = out_3.flatten_outer_dims().rearrange("(p i) c -> p i c", i=NT)
+
+    with ExitStack() as ctx:
+        keep = ctx.enter_context(tc.tile_pool(name="keep", bufs=1))
+        xgp = ctx.enter_context(tc.tile_pool(name="xgp", bufs=3))
+        wup = ctx.enter_context(tc.tile_pool(name="wup", bufs=3))
+        wgp = ctx.enter_context(tc.tile_pool(name="wgp", bufs=3))
+        stage = ctx.enter_context(tc.tile_pool(name="stage", bufs=10))
+        rot = ctx.enter_context(tc.tile_pool(name="rot", bufs=1))
+        psum = ctx.enter_context(tc.psum_pool(name="psum", bufs=8))
+        ctx.enter_context(tc.manual_schedule())
+
+        ident = keep.tile([P, P], F32, name="ident")
+        ones = keep.tile([P, P], BF16, name="ones")
+        gsrc = keep.tile([P, 2 * D], BF16, name="gsrc")
+        gains = keep.tile([P, 2, D], F32, name="gains")
+        tab = keep.tile([P, 3, NT, D // 2], BF16, name="tab")
+        x_codes = keep.tile([P, NT, 2, P], U32, name="x_codes", align_bytes=64)
+        x_scales = keep.tile([P, NT, 2, P], U8, name="x_scales", align_bytes=64)
+        w_codes = keep.tile([P, 2, 2 * E], U32, name="w_codes", align_bytes=64)
+        w_scales = keep.tile([P, 2, 2 * E], U8, name="w_scales", align_bytes=64)
+        wq_codes = keep.tile([P, 2, D], U32, name="wq_codes", align_bytes=64)
+        wq_scales = keep.tile([P, 2, D], U8, name="wq_scales", align_bytes=64)
+        wq_grp = keep.tile([P, 2, D, 4], BF16, name="wq_grp", align_bytes=64)
+        wv_raw = keep.tile([P, 4, 2, VW], BF16, name="wv_raw")
+        z = keep.tile([P, NT, D], F32, name="z")
+        x_raw = [keep.tile([P, 2, 1024], BF16, name="x_raw%d" % d) for d in range(4)]
+
+        make_identity(nc, ident[:])
+        nc.gpsimd.memset(ones[:], 1.0)
+        nc.gpsimd.memset(gsrc[:], 0.0)
+
+        wu_raw = []
+
+        def load_wu(c):
+            t = wup.tile([P, 4, 2, CH], BF16, name="wu_raw%d" % c, tag="wu_raw")
+            for e in range(2):
+                nc.sync.dma_start(out=t[:, :, e, :], in_=w_by_e[e, :, :, c * CH : (c + 1) * CH])
+            wu_raw.append(t)
+
+        load_wu(0)
+        for d in range(4):
+            nc.sync.dma_start(out=x_raw[d][:], in_=x_dram[:, 2 * d : 2 * d + 2, :])
+        load_wu(1)
+        load_wu(2)
+        for a in range(4):
+            nc.sync.dma_start(out=wv_raw[:, a, :, :], in_=w_by_a[a, :, :, E : E + VW])
+        nc.sync.dma_start(out=tab[:, 0, :, :], in_=cos_dram)
+        nc.sync.dma_start(out=tab[:, 1, :, :], in_=sin_dram)
+        nc.sync.dma_start(out=tab[:, 2, :, :], in_=cos_dram)
+        nc.sync.dma_start(out=gsrc[0:1, 0:D], in_=q_scale.rearrange("(o d) -> o d", o=1))
+        nc.sync.dma_start(out=gsrc[0:1, D : 2 * D], in_=k_scale.rearrange("(o d) -> o d", o=1))
+
+        def w_src(c, g):
+            if c < 3:
+                return wu_raw[c][:, 2 * g : 2 * g + 2].rearrange("p u e n -> p (u e) n")
+            lo = (c - 3) * CH
+            return wv_raw[:, 2 * g : 2 * g + 2, :, lo : lo + CH].rearrange("p u e n -> p (u e) n")
+
+        grouped = {}
+
+        def regroup(job):
+            if job == "qk":
+                src = wv_raw[:, :, :, E : E + D].rearrange("p (g u) e n -> p g (u e) n", g=2)
+                nc.vector.tensor_copy(out=wq_grp[:], in_=src.rearrange("p g t n -> p g n t"))
+                return
+            c, g = job
+            t = wgp.tile([P, CH, 4], BF16, name="wgrp%d_%d" % (c, g), tag="wgrp", align_bytes=64)
+            nc.vector.tensor_copy(
+                out=t[:].rearrange("p (n i) t -> p n t i", i=4),
+                in_=w_src(c, g).rearrange("p t (n i) -> p n t i", i=4),
+            )
+            grouped[job] = t
+
+        def quantise(job):
+            if job == "qk":
+                nc.vector.quantize_mx(
+                    out=wq_codes[:].rearrange("p g n -> p (g n)").bitcast(FP8X4),
+                    scales=wq_scales[:].rearrange("p g n -> p (g n)"),
+                    in_=wq_grp[:].rearrange("p g n t -> p (g n t)"),
+                )
+                return
+            c, g = job
+            cols = slice(c * CH, (c + 1) * CH)
+            nc.vector.quantize_mx(
+                out=w_codes[:, g, cols].bitcast(FP8X4),
+                scales=w_scales[:, g, cols],
+                in_=grouped[job][:].rearrange("p n t -> p (n t)"),
+            )
+
+        def w_jobs(jobs):
+            for n, job in enumerate(jobs):
+                regroup(job)
+                if n > 0:
+                    quantise(jobs[n - 1])
+            quantise(jobs[-1])
+
+        xg = {}
+
+        def x_transpose(i):
+            d, r = divmod(i, 2)
+            if r == 0:
+                xg[d] = xgp.tile([P, 2, 2, P, 4], BF16, name="xg%d" % d, tag="xg", align_bytes=64)
+            xt = psum.tile([P, 4, P], F32, name="xt%d" % i, tag="bank")
+            words = x_raw[d][:, r, :].bitcast(F32)
+            for b in range(4):
+                nc.tensor.transpose(xt[:, b, :], words[:, b * P : (b + 1) * P], ident[:])
+            nc.scalar.copy(
+                out=xg[d][:, r, :, :, :].bitcast(F32),
+                in_=xt[:].rearrange("p (g u) r -> p g r u", u=2),
+            )
+
+        def x_quantise(d):
+            nc.vector.quantize_mx(
+                out=x_codes[:, 2 * d : 2 * d + 2].rearrange("p i g r -> p (i g r)").bitcast(FP8X4),
+                scales=x_scales[:, 2 * d : 2 * d + 2].rearrange("p i g r -> p (i g r)"),
+                in_=xg[d][:].rearrange("p i g r t -> p (i g r t)"),
+            )
+
+        def mx(acc, i, codes, scales):
+            for g in range(2):
+                nc.tensor.matmul_mx(
+                    out=acc,
+                    lhsT=x_codes[:, i, g, :].bitcast(FP8X4),
+                    lhsT_scale=x_scales[:, i, g, :],
+                    rhs=codes(g).bitcast(FP8X4),
+                    rhs_scale=scales(g),
+                    start=(g == 0),
+                    stop=(g == 1),
+                )
+
+        def mx_chunk(i, c, dst):
+            cols = slice(c * CH, (c + 1) * CH)
+            acc = psum.tile([P, CH], F32, name="acc%d_%d" % (c, i), tag="bank")
+            mx(acc[:], i, lambda g: w_codes[:, g, cols], lambda g: w_scales[:, g, cols])
+            lo = (c % 3) * CH
+            nc.scalar.activation(out=dst[:, lo : lo + CH], in_=acc[:], func=SILU)
+
+        regroup((0, 0))
+        regroup((0, 1))
+        quantise((0, 0))
+        x_transpose(0)
+        x_transpose(1)
+        x_quantise(0)
+        quantise((0, 1))
+        for d in range(1, 4):
+            x_transpose(2 * d)
+            x_transpose(2 * d + 1)
+            x_quantise(d)
+
+        u_sb = [stage.tile([P, E], F32, name="u_sb%d" % i, tag="stage") for i in range(NT)]
+        for c in range(3):
+            if c > 0:
+                w_jobs([(c, 0), (c, 1)])
+            for i in range(NT):
+                mx_chunk(i, c, u_sb[i])
+                if c == 2:
+                    nc.sync.dma_start(out=u_dram[i, :, :], in_=u_sb[i][:])
+
+        w_jobs([(3, 0), (4, 0), (5, 0), "qk", (3, 1), (4, 1), (5, 1)])
+
+        gps = psum.tile([P, CH], F32, name="gps", tag="bank")
+        nc.tensor.matmul(out=gps[:, 0 : 2 * D], lhsT=ones[:], rhs=gsrc[:], start=True, stop=True)
+        nc.scalar.copy(out=gains[:].rearrange("p s d -> p (s d)"), in_=gps[:, 0 : 2 * D])
+        for h in range(2):
+            zb = psum.tile([P, 4, D], F32, name="zb%d" % h, tag="bank")
+            for r in range(4):
+                mx(zb[:, r, :], 4 * h + r, lambda g: wq_codes[:, g, :], lambda g: wq_scales[:, g, :])
+            nc.scalar.activation(out=z[:, 4 * h : 4 * h + 4, :], in_=zb[:], func=SILU)
+
+        for i in range(NT):
+            v_sb = stage.tile([P, E], F32, name="v_sb%d" % i, tag="stage")
+            for c in range(3, 6):
+                mx_chunk(i, c, v_sb)
+            nc.sync.dma_start(out=v_dram[i, :, :], in_=v_sb[:])
+
+        for s, dram in enumerate((q_dram, k_dram)):
+            y = rot.tile([P, NT, D], F32, name="y%d" % s, tag="y")
+            a_t = rot.tile([P, NT, 2, D // 2], F32, name="a%d" % s, tag="a", bufs=2)
+            b_t = rot.tile([P, NT, 2, D // 2], F32, name="b%d" % s, tag="b")
+            nc.vector.tensor_tensor(
+                out=y[:], in0=z[:], in1=gains[:, s, :].unsqueeze(1).to_broadcast([P, NT, D]), op=MULT
+            )
+            pairs = y[:].rearrange("p i (j e) -> p i e j", e=2)
+            shape = [P, NT, 2, D // 2]
+            nc.vector.tensor_tensor(
+                out=a_t[:],
+                in0=pairs[:, :, 0, :].unsqueeze(2).to_broadcast(shape),
+                in1=tab[:, 0:2].rearrange("p h i j -> p i h j"),
+                op=MULT,
+            )
+            nc.vector.tensor_tensor(
+                out=b_t[:],
+                in0=pairs[:, :, 1, :].unsqueeze(2).to_broadcast(shape),
+                in1=tab[:, 1:3].rearrange("p h i j -> p i h j"),
+                op=MULT,
+            )
+            nc.vector.tensor_tensor(out=a_t[:, :, 0, :], in0=a_t[:, :, 0, :], in1=b_t[:, :, 0, :], op=SUB)
+            nc.vector.tensor_tensor(out=a_t[:, :, 1, :], in0=a_t[:, :, 1, :], in1=b_t[:, :, 1, :], op=ADD)
+            nc.sync.dma_start(out=dram, in_=a_t[:].rearrange("p i h j -> p i (h j)"))

@@ -76,10 +76,12 @@ def tile_gatedattentionunit_pa_kernel(
             wu_raw.append(t)
 
         load_wu(0)
-        for d in range(4):
+        for d in range(2):
             nc.sync.dma_start(out=x_raw[d][:], in_=x_dram[:, 2 * d : 2 * d + 2, :])
         load_wu(1)
         load_wu(2)
+        for d in range(2, 4):
+            nc.sync.dma_start(out=x_raw[d][:], in_=x_dram[:, 2 * d : 2 * d + 2, :])
         for a in range(4):
             nc.sync.dma_start(out=wv_raw[:, a, :, :], in_=w_by_a[a, :, :, E : E + VW])
         nc.sync.dma_start(out=tab[:, 0, :, :], in_=cos_dram)
@@ -180,21 +182,47 @@ def tile_gatedattentionunit_pa_kernel(
         x_transpose(1)
         x_quantise(0)
         quantise((0, 1))
-        for d in range(1, 4):
-            x_transpose(2 * d)
-            x_transpose(2 * d + 1)
-            x_quantise(d)
+        x_transpose(2)
+        x_transpose(3)
+        x_quantise(1)
 
-        u_sb = [stage.tile([P, E], F32, name="u_sb%d" % i, tag="stage") for i in range(NT)]
-        for c in range(3):
-            if c > 0:
-                w_jobs([(c, 0), (c, 1)])
-            for i in range(NT):
-                mx_chunk(i, c, u_sb[i])
-                if c == 2:
-                    nc.sync.dma_start(out=u_dram[i, :, :], in_=u_sb[i][:])
+        u_sb = [stage.tile([P, E], F32, name="u_sb%d" % i, tag="stage") for i in range(4)]
+        for i in range(4):
+            mx_chunk(i, 0, u_sb[i])
+        w_jobs([(1, 0), (1, 1)])
+        for i in range(4):
+            mx_chunk(i, 1, u_sb[i])
+        x_transpose(4)
+        x_transpose(5)
+        w_jobs([(2, 0), (2, 1)])
+        x_quantise(2)
+        for i in range(4):
+            mx_chunk(i, 2, u_sb[i])
+            nc.sync.dma_start(out=u_dram[i, :, :], in_=u_sb[i][:])
+        x_transpose(6)
+        x_transpose(7)
 
-        w_jobs([(3, 0), (4, 0), (5, 0), "qk", (3, 1), (4, 1), (5, 1)])
+        regroup((3, 0))
+        regroup((4, 0))
+        quantise((3, 0))
+        x_quantise(3)
+        regroup((5, 0))
+        quantise((4, 0))
+        regroup("qk")
+        quantise((5, 0))
+        regroup((3, 1))
+        quantise("qk")
+        regroup((4, 1))
+        quantise((3, 1))
+        regroup((5, 1))
+        quantise((4, 1))
+        quantise((5, 1))
+
+        for i in range(4, NT):
+            u_t = stage.tile([P, E], F32, name="u_sb%d" % i, tag="stage")
+            for c in range(3):
+                mx_chunk(i, c, u_t)
+            nc.sync.dma_start(out=u_dram[i, :, :], in_=u_t[:])
 
         gps = psum.tile([P, CH], F32, name="gps", tag="bank")
         nc.tensor.matmul(out=gps[:, 0 : 2 * D], lhsT=ones[:], rhs=gsrc[:], start=True, stop=True)

@@ -19,6 +19,7 @@ E = 1536
 D = 128
 CH = 512
 VW = E + D
+EARLY = 4
 
 FLOPS = 2 * 1024 * 1024 * 3200
 
@@ -42,7 +43,7 @@ def tile_gatedattentionunit_pa_kernel(
         xgp = ctx.enter_context(tc.tile_pool(name="xgp", bufs=3))
         wup = ctx.enter_context(tc.tile_pool(name="wup", bufs=3))
         wgp = ctx.enter_context(tc.tile_pool(name="wgp", bufs=3))
-        stage = ctx.enter_context(tc.tile_pool(name="stage", bufs=10))
+        stage = ctx.enter_context(tc.tile_pool(name="stage", bufs=12))
         rot = ctx.enter_context(tc.tile_pool(name="rot", bufs=1))
         psum = ctx.enter_context(tc.psum_pool(name="psum", bufs=8))
         ctx.enter_context(tc.manual_schedule())
@@ -76,12 +77,10 @@ def tile_gatedattentionunit_pa_kernel(
             wu_raw.append(t)
 
         load_wu(0)
-        for d in range(2):
+        for d in range(4):
             nc.sync.dma_start(out=x_raw[d][:], in_=x_dram[:, 2 * d : 2 * d + 2, :])
         load_wu(1)
         load_wu(2)
-        for d in range(2, 4):
-            nc.sync.dma_start(out=x_raw[d][:], in_=x_dram[:, 2 * d : 2 * d + 2, :])
         for a in range(4):
             nc.sync.dma_start(out=wv_raw[:, a, :, :], in_=w_by_a[a, :, :, E : E + VW])
         nc.sync.dma_start(out=tab[:, 0, :, :], in_=cos_dram)
@@ -182,47 +181,45 @@ def tile_gatedattentionunit_pa_kernel(
         x_transpose(1)
         x_quantise(0)
         quantise((0, 1))
-        x_transpose(2)
-        x_transpose(3)
-        x_quantise(1)
+        for d in range(1, 4):
+            x_transpose(2 * d)
+            x_transpose(2 * d + 1)
+            x_quantise(d)
 
-        u_sb = [stage.tile([P, E], F32, name="u_sb%d" % i, tag="stage") for i in range(4)]
-        for i in range(4):
+        u_sb = [stage.tile([P, E], F32, name="u_sb%d" % i, tag="stage") for i in range(NT)]
+        for i in range(NT):
             mx_chunk(i, 0, u_sb[i])
         w_jobs([(1, 0), (1, 1)])
-        for i in range(4):
+        for i in range(NT):
             mx_chunk(i, 1, u_sb[i])
-        x_transpose(4)
-        x_transpose(5)
+            if i < EARLY:
+                nc.sync.dma_start(out=u_dram[i, :, 0 : 2 * CH], in_=u_sb[i][:, 0 : 2 * CH])
         w_jobs([(2, 0), (2, 1)])
-        x_quantise(2)
-        for i in range(4):
+        for i in range(NT):
             mx_chunk(i, 2, u_sb[i])
-            nc.sync.dma_start(out=u_dram[i, :, :], in_=u_sb[i][:])
-        x_transpose(6)
-        x_transpose(7)
+            if i < EARLY:
+                nc.sync.dma_start(out=u_dram[i, :, 2 * CH : E], in_=u_sb[i][:, 2 * CH : E])
+            else:
+                nc.sync.dma_start(out=u_dram[i, :, :], in_=u_sb[i][:])
 
         regroup((3, 0))
         regroup((4, 0))
         quantise((3, 0))
-        x_quantise(3)
-        regroup((5, 0))
+        regroup((3, 1))
         quantise((4, 0))
         regroup("qk")
-        quantise((5, 0))
-        regroup((3, 1))
-        quantise("qk")
-        regroup((4, 1))
         quantise((3, 1))
-        regroup((5, 1))
+        regroup((4, 1))
+        quantise("qk")
+        regroup((5, 0))
         quantise((4, 1))
+        regroup((5, 1))
+        quantise((5, 0))
         quantise((5, 1))
 
-        for i in range(4, NT):
-            u_t = stage.tile([P, E], F32, name="u_sb%d" % i, tag="stage")
-            for c in range(3):
-                mx_chunk(i, c, u_t)
-            nc.sync.dma_start(out=u_dram[i, :, :], in_=u_t[:])
+        v_sb = [stage.tile([P, E], F32, name="v_sb%d" % i, tag="stage") for i in range(4)]
+        for i in range(4):
+            mx_chunk(i, 3, v_sb[i])
 
         gps = psum.tile([P, CH], F32, name="gps", tag="bank")
         nc.tensor.matmul(out=gps[:, 0 : 2 * D], lhsT=ones[:], rhs=gsrc[:], start=True, stop=True)
@@ -233,13 +230,13 @@ def tile_gatedattentionunit_pa_kernel(
                 mx(zb[:, r, :], 4 * h + r, lambda g: wq_codes[:, g, :], lambda g: wq_scales[:, g, :])
             nc.scalar.activation(out=z[:, 4 * h : 4 * h + 4, :], in_=zb[:], func=SILU)
 
-        for i in range(NT):
-            v_sb = stage.tile([P, E], F32, name="v_sb%d" % i, tag="stage")
-            for c in range(3, 6):
-                mx_chunk(i, c, v_sb)
-            nc.sync.dma_start(out=v_dram[i, :, :], in_=v_sb[:])
+        for i in range(4):
+            mx_chunk(i, 4, v_sb[i])
+        for i in range(4):
+            mx_chunk(i, 5, v_sb[i])
+            nc.sync.dma_start(out=v_dram[i, :, :], in_=v_sb[i][:])
 
-        for s, dram in enumerate((q_dram, k_dram)):
+        def rotate(s, dram):
             y = rot.tile([P, NT, D], F32, name="y%d" % s, tag="y")
             a_t = rot.tile([P, NT, 2, D // 2], F32, name="a%d" % s, tag="a", bufs=2)
             b_t = rot.tile([P, NT, 2, D // 2], F32, name="b%d" % s, tag="b")
@@ -263,3 +260,16 @@ def tile_gatedattentionunit_pa_kernel(
             nc.vector.tensor_tensor(out=a_t[:, :, 0, :], in0=a_t[:, :, 0, :], in1=b_t[:, :, 0, :], op=SUB)
             nc.vector.tensor_tensor(out=a_t[:, :, 1, :], in0=a_t[:, :, 1, :], in1=b_t[:, :, 1, :], op=ADD)
             nc.sync.dma_start(out=dram, in_=a_t[:].rearrange("p i h j -> p i (h j)"))
+
+        def v_tile(i):
+            v_t = stage.tile([P, E], F32, name="v_sb%d" % i, tag="stage")
+            for c in range(3, 6):
+                mx_chunk(i, c, v_t)
+            nc.sync.dma_start(out=v_dram[i, :, :], in_=v_t[:])
+
+        rotate(0, q_dram)
+        v_tile(4)
+        v_tile(5)
+        v_tile(6)
+        rotate(1, k_dram)
+        v_tile(7)

@@ -19,7 +19,6 @@ E = 1536
 D = 128
 CH = 512
 VW = E + D
-EARLY = 4
 
 FLOPS = 2 * 1024 * 1024 * 3200
 
@@ -33,17 +32,16 @@ def tile_gatedattentionunit_pa_kernel(
     sin_dram = sin.flatten_outer_dims().rearrange("(p i) j -> p i j", i=NT)
     w_by_e = W_i.rearrange("(a q e) n -> e q a n", a=4, e=2)
     w_by_a = W_i.rearrange("(a q e) n -> a q e n", a=4, e=2)
-    u_dram = out_0.flatten_outer_dims().rearrange("(p i) c -> i p c", i=NT)
-    v_dram = out_1.flatten_outer_dims().rearrange("(p i) c -> i p c", i=NT)
+    u_dram = out_0.flatten_outer_dims().rearrange("(p j r) c -> j p r c", j=NT // 2, r=2)
+    v_dram = out_1.flatten_outer_dims().rearrange("(p j r) c -> j p r c", j=NT // 2, r=2)
     q_dram = out_2.flatten_outer_dims().rearrange("(p i) c -> p i c", i=NT)
     k_dram = out_3.flatten_outer_dims().rearrange("(p i) c -> p i c", i=NT)
 
     with ExitStack() as ctx:
         keep = ctx.enter_context(tc.tile_pool(name="keep", bufs=1))
         xgp = ctx.enter_context(tc.tile_pool(name="xgp", bufs=3))
-        wup = ctx.enter_context(tc.tile_pool(name="wup", bufs=3))
         wgp = ctx.enter_context(tc.tile_pool(name="wgp", bufs=3))
-        stage = ctx.enter_context(tc.tile_pool(name="stage", bufs=12))
+        stage = ctx.enter_context(tc.tile_pool(name="stage", bufs=6))
         rot = ctx.enter_context(tc.tile_pool(name="rot", bufs=1))
         psum = ctx.enter_context(tc.psum_pool(name="psum", bufs=8))
         ctx.enter_context(tc.manual_schedule())
@@ -52,7 +50,7 @@ def tile_gatedattentionunit_pa_kernel(
         ones = keep.tile([P, P], BF16, name="ones")
         gsrc = keep.tile([P, 2 * D], BF16, name="gsrc")
         gains = keep.tile([P, 2, D], F32, name="gains")
-        tab = keep.tile([P, 3, NT, D // 2], BF16, name="tab")
+        tab = keep.tile([P, 2, NT, D // 2], BF16, name="tab")
         x_codes = keep.tile([P, NT, 2, P], U32, name="x_codes", align_bytes=64)
         x_scales = keep.tile([P, NT, 2, P], U8, name="x_scales", align_bytes=64)
         w_codes = keep.tile([P, 2, 2 * E], U32, name="w_codes", align_bytes=64)
@@ -60,6 +58,8 @@ def tile_gatedattentionunit_pa_kernel(
         wq_codes = keep.tile([P, 2, D], U32, name="wq_codes", align_bytes=64)
         wq_scales = keep.tile([P, 2, D], U8, name="wq_scales", align_bytes=64)
         wq_grp = keep.tile([P, 2, D, 4], BF16, name="wq_grp", align_bytes=64)
+        w0_raw = keep.tile([P, 4, 2, CH], BF16, name="w0_raw")
+        w12_raw = keep.tile([P, 4, 2, 2 * CH], BF16, name="w12_raw")
         wv_raw = keep.tile([P, 4, 2, VW], BF16, name="wv_raw")
         z = keep.tile([P, NT, D], F32, name="z")
         x_raw = [keep.tile([P, 2, 1024], BF16, name="x_raw%d" % d) for d in range(4)]
@@ -68,32 +68,27 @@ def tile_gatedattentionunit_pa_kernel(
         nc.gpsimd.memset(ones[:], 1.0)
         nc.gpsimd.memset(gsrc[:], 0.0)
 
-        wu_raw = []
-
-        def load_wu(c):
-            t = wup.tile([P, 4, 2, CH], BF16, name="wu_raw%d" % c, tag="wu_raw")
-            for e in range(2):
-                nc.sync.dma_start(out=t[:, :, e, :], in_=w_by_e[e, :, :, c * CH : (c + 1) * CH])
-            wu_raw.append(t)
-
-        load_wu(0)
+        for e in range(2):
+            nc.sync.dma_start(out=w0_raw[:, :, e, :], in_=w_by_e[e, :, :, 0:CH])
         for d in range(4):
             nc.sync.dma_start(out=x_raw[d][:], in_=x_dram[:, 2 * d : 2 * d + 2, :])
-        load_wu(1)
-        load_wu(2)
+        for a in range(4):
+            nc.sync.dma_start(out=w12_raw[:, a, :, :], in_=w_by_a[a, :, :, CH:E])
         for a in range(4):
             nc.sync.dma_start(out=wv_raw[:, a, :, :], in_=w_by_a[a, :, :, E : E + VW])
         nc.sync.dma_start(out=tab[:, 0, :, :], in_=cos_dram)
         nc.sync.dma_start(out=tab[:, 1, :, :], in_=sin_dram)
-        nc.sync.dma_start(out=tab[:, 2, :, :], in_=cos_dram)
         nc.sync.dma_start(out=gsrc[0:1, 0:D], in_=q_scale.rearrange("(o d) -> o d", o=1))
         nc.sync.dma_start(out=gsrc[0:1, D : 2 * D], in_=k_scale.rearrange("(o d) -> o d", o=1))
 
         def w_src(c, g):
-            if c < 3:
-                return wu_raw[c][:, 2 * g : 2 * g + 2].rearrange("p u e n -> p (u e) n")
-            lo = (c - 3) * CH
-            return wv_raw[:, 2 * g : 2 * g + 2, :, lo : lo + CH].rearrange("p u e n -> p (u e) n")
+            if c == 0:
+                raw, lo = w0_raw, 0
+            elif c < 3:
+                raw, lo = w12_raw, (c - 1) * CH
+            else:
+                raw, lo = wv_raw, (c - 3) * CH
+            return raw[:, 2 * g : 2 * g + 2, :, lo : lo + CH].rearrange("p u e n -> p (u e) n")
 
         grouped = {}
 
@@ -125,13 +120,6 @@ def tile_gatedattentionunit_pa_kernel(
                 scales=w_scales[:, g, cols],
                 in_=grouped[job][:].rearrange("p n t -> p (n t)"),
             )
-
-        def w_jobs(jobs):
-            for n, job in enumerate(jobs):
-                regroup(job)
-                if n > 0:
-                    quantise(jobs[n - 1])
-            quantise(jobs[-1])
 
         xg = {}
 
@@ -167,12 +155,15 @@ def tile_gatedattentionunit_pa_kernel(
                     stop=(g == 1),
                 )
 
-        def mx_chunk(i, c, dst):
+        def mx_chunk(i, c, pair):
             cols = slice(c * CH, (c + 1) * CH)
             acc = psum.tile([P, CH], F32, name="acc%d_%d" % (c, i), tag="bank")
             mx(acc[:], i, lambda g: w_codes[:, g, cols], lambda g: w_scales[:, g, cols])
             lo = (c % 3) * CH
-            nc.scalar.activation(out=dst[:, lo : lo + CH], in_=acc[:], func=SILU)
+            nc.scalar.activation(out=pair[:, i % 2, lo : lo + CH], in_=acc[:], func=SILU)
+
+        def pair_tile(name):
+            return stage.tile([P, 2, E], F32, name=name, tag="stage")
 
         regroup((0, 0))
         regroup((0, 1))
@@ -186,21 +177,28 @@ def tile_gatedattentionunit_pa_kernel(
             x_transpose(2 * d + 1)
             x_quantise(d)
 
-        u_sb = [stage.tile([P, E], F32, name="u_sb%d" % i, tag="stage") for i in range(NT)]
+        u_sb = [pair_tile("u_sb%d" % j) for j in range(NT // 2)]
         for i in range(NT):
-            mx_chunk(i, 0, u_sb[i])
-        w_jobs([(1, 0), (1, 1)])
-        for i in range(NT):
-            mx_chunk(i, 1, u_sb[i])
-            if i < EARLY:
-                nc.sync.dma_start(out=u_dram[i, :, 0 : 2 * CH], in_=u_sb[i][:, 0 : 2 * CH])
-        w_jobs([(2, 0), (2, 1)])
-        for i in range(NT):
-            mx_chunk(i, 2, u_sb[i])
-            if i < EARLY:
-                nc.sync.dma_start(out=u_dram[i, :, 2 * CH : E], in_=u_sb[i][:, 2 * CH : E])
-            else:
-                nc.sync.dma_start(out=u_dram[i, :, :], in_=u_sb[i][:])
+            mx_chunk(i, 0, u_sb[i // 2])
+        regroup((1, 0))
+        regroup((2, 0))
+        regroup((1, 1))
+        quantise((1, 0))
+        quantise((1, 1))
+        regroup((2, 1))
+        quantise((2, 0))
+        quantise((2, 1))
+        for i in range(4):
+            mx_chunk(i, 1, u_sb[i // 2])
+        for i in range(4):
+            mx_chunk(i, 2, u_sb[i // 2])
+            if i % 2 == 1:
+                nc.sync.dma_start(out=u_dram[i // 2, :, :, :], in_=u_sb[i // 2][:])
+        for i in range(4, NT):
+            mx_chunk(i, 1, u_sb[i // 2])
+            mx_chunk(i, 2, u_sb[i // 2])
+            if i % 2 == 1:
+                nc.sync.dma_start(out=u_dram[i // 2, :, :, :], in_=u_sb[i // 2][:])
 
         regroup((3, 0))
         regroup((4, 0))
@@ -217,9 +215,9 @@ def tile_gatedattentionunit_pa_kernel(
         quantise((5, 0))
         quantise((5, 1))
 
-        v_sb = [stage.tile([P, E], F32, name="v_sb%d" % i, tag="stage") for i in range(4)]
+        v_sb = [pair_tile("v_sb%d" % j) for j in range(2)]
         for i in range(4):
-            mx_chunk(i, 3, v_sb[i])
+            mx_chunk(i, 3, v_sb[i // 2])
 
         gps = psum.tile([P, CH], F32, name="gps", tag="bank")
         nc.tensor.matmul(out=gps[:, 0 : 2 * D], lhsT=ones[:], rhs=gsrc[:], start=True, stop=True)
@@ -231,45 +229,42 @@ def tile_gatedattentionunit_pa_kernel(
             nc.scalar.activation(out=z[:, 4 * h : 4 * h + 4, :], in_=zb[:], func=SILU)
 
         for i in range(4):
-            mx_chunk(i, 4, v_sb[i])
+            mx_chunk(i, 4, v_sb[i // 2])
         for i in range(4):
-            mx_chunk(i, 5, v_sb[i])
-            nc.sync.dma_start(out=v_dram[i, :, :], in_=v_sb[i][:])
+            mx_chunk(i, 5, v_sb[i // 2])
+            if i % 2 == 1:
+                nc.sync.dma_start(out=v_dram[i // 2, :, :, :], in_=v_sb[i // 2][:])
 
         def rotate(s, dram):
             y = rot.tile([P, NT, D], F32, name="y%d" % s, tag="y")
-            a_t = rot.tile([P, NT, 2, D // 2], F32, name="a%d" % s, tag="a", bufs=2)
-            b_t = rot.tile([P, NT, 2, D // 2], F32, name="b%d" % s, tag="b")
+            m_cos = rot.tile([P, NT, 2, D // 2], F32, name="mc%d" % s, tag="mc", bufs=2)
+            m_sin = rot.tile([P, NT, 2, D // 2], F32, name="ms%d" % s, tag="ms")
             nc.vector.tensor_tensor(
                 out=y[:], in0=z[:], in1=gains[:, s, :].unsqueeze(1).to_broadcast([P, NT, D]), op=MULT
             )
             pairs = y[:].rearrange("p i (j e) -> p i e j", e=2)
             shape = [P, NT, 2, D // 2]
             nc.vector.tensor_tensor(
-                out=a_t[:],
-                in0=pairs[:, :, 0, :].unsqueeze(2).to_broadcast(shape),
-                in1=tab[:, 0:2].rearrange("p h i j -> p i h j"),
-                op=MULT,
+                out=m_cos[:], in0=pairs, in1=tab[:, 0, :, :].unsqueeze(2).to_broadcast(shape), op=MULT
             )
             nc.vector.tensor_tensor(
-                out=b_t[:],
-                in0=pairs[:, :, 1, :].unsqueeze(2).to_broadcast(shape),
-                in1=tab[:, 1:3].rearrange("p h i j -> p i h j"),
-                op=MULT,
+                out=m_sin[:], in0=pairs, in1=tab[:, 1, :, :].unsqueeze(2).to_broadcast(shape), op=MULT
             )
-            nc.vector.tensor_tensor(out=a_t[:, :, 0, :], in0=a_t[:, :, 0, :], in1=b_t[:, :, 0, :], op=SUB)
-            nc.vector.tensor_tensor(out=a_t[:, :, 1, :], in0=a_t[:, :, 1, :], in1=b_t[:, :, 1, :], op=ADD)
-            nc.sync.dma_start(out=dram, in_=a_t[:].rearrange("p i h j -> p i (h j)"))
-
-        def v_tile(i):
-            v_t = stage.tile([P, E], F32, name="v_sb%d" % i, tag="stage")
-            for c in range(3, 6):
-                mx_chunk(i, c, v_t)
-            nc.sync.dma_start(out=v_dram[i, :, :], in_=v_t[:])
+            nc.vector.tensor_tensor(out=m_cos[:, :, 0, :], in0=m_cos[:, :, 0, :], in1=m_sin[:, :, 1, :], op=SUB)
+            nc.vector.tensor_tensor(out=m_cos[:, :, 1, :], in0=m_cos[:, :, 1, :], in1=m_sin[:, :, 0, :], op=ADD)
+            nc.sync.dma_start(out=dram, in_=m_cos[:].rearrange("p i h j -> p i (h j)"))
 
         rotate(0, q_dram)
-        v_tile(4)
-        v_tile(5)
-        v_tile(6)
+        v45 = pair_tile("v_sb2")
+        for i in (4, 5):
+            for c in range(3, 6):
+                mx_chunk(i, c, v45)
+        nc.sync.dma_start(out=v_dram[2, :, :, :], in_=v45[:])
+        v67 = pair_tile("v_sb3")
+        for c in range(3, 6):
+            mx_chunk(6, c, v67)
+        nc.sync.dma_start(out=v_dram[3, :, 0, :], in_=v67[:, 0, :])
         rotate(1, k_dram)
-        v_tile(7)
+        for c in range(3, 6):
+            mx_chunk(7, c, v67)
+        nc.sync.dma_start(out=v_dram[3, :, 1, :], in_=v67[:, 1, :])

@@ -30,7 +30,6 @@ def tile_gatedattentionunit_pa_kernel(
     x_dram = hidden_states.flatten_outer_dims().rearrange("(p i) k -> p i k", i=NT)
     cos_dram = cos.flatten_outer_dims().rearrange("(p i) j -> p i j", i=NT)
     sin_dram = sin.flatten_outer_dims().rearrange("(p i) j -> p i j", i=NT)
-    w_by_e = W_i.rearrange("(a q e) n -> e q a n", a=4, e=2)
     w_by_a = W_i.rearrange("(a q e) n -> a q e n", a=4, e=2)
     u_dram = out_0.flatten_outer_dims().rearrange("(p j r) c -> j p r c", j=NT // 2, r=2)
     v_dram = out_1.flatten_outer_dims().rearrange("(p j r) c -> j p r c", j=NT // 2, r=2)
@@ -58,22 +57,27 @@ def tile_gatedattentionunit_pa_kernel(
         wq_codes = keep.tile([P, 2, D], U32, name="wq_codes", align_bytes=64)
         wq_scales = keep.tile([P, 2, D], U8, name="wq_scales", align_bytes=64)
         wq_grp = keep.tile([P, 2, D, 4], BF16, name="wq_grp", align_bytes=64)
-        w0_raw = keep.tile([P, 4, 2, CH], BF16, name="w0_raw")
-        w12_raw = keep.tile([P, 4, 2, 2 * CH], BF16, name="w12_raw")
+        wu_raw = keep.tile([P, 4, 2, E], BF16, name="wu_raw")
         wv_raw = keep.tile([P, 4, 2, VW], BF16, name="wv_raw")
         z = keep.tile([P, NT, D], F32, name="z")
-        x_raw = [keep.tile([P, 2, 1024], BF16, name="x_raw%d" % d) for d in range(4)]
+        x_raw = [keep.tile([P, 4, 1024], BF16, name="x_raw%d" % h) for h in range(2)]
 
         make_identity(nc, ident[:])
         nc.gpsimd.memset(ones[:], 1.0)
         nc.gpsimd.memset(gsrc[:], 0.0)
 
-        for e in range(2):
-            nc.sync.dma_start(out=w0_raw[:, :, e, :], in_=w_by_e[e, :, :, 0:CH])
-        for d in range(4):
-            nc.sync.dma_start(out=x_raw[d][:], in_=x_dram[:, 2 * d : 2 * d + 2, :])
-        for a in range(4):
-            nc.sync.dma_start(out=w12_raw[:, a, :, :], in_=w_by_a[a, :, :, CH:E])
+        def load_wu(a):
+            nc.sync.dma_start(out=wu_raw[:, a, :, :], in_=w_by_a[a, :, :, 0:E])
+
+        def load_x(h):
+            nc.sync.dma_start(out=x_raw[h][:], in_=x_dram[:, 4 * h : 4 * h + 4, :])
+
+        load_wu(0)
+        load_wu(1)
+        load_x(0)
+        load_wu(2)
+        load_wu(3)
+        load_x(1)
         for a in range(4):
             nc.sync.dma_start(out=wv_raw[:, a, :, :], in_=w_by_a[a, :, :, E : E + VW])
         nc.sync.dma_start(out=tab[:, 0, :, :], in_=cos_dram)
@@ -82,10 +86,8 @@ def tile_gatedattentionunit_pa_kernel(
         nc.sync.dma_start(out=gsrc[0:1, D : 2 * D], in_=k_scale.rearrange("(o d) -> o d", o=1))
 
         def w_src(c, g):
-            if c == 0:
-                raw, lo = w0_raw, 0
-            elif c < 3:
-                raw, lo = w12_raw, (c - 1) * CH
+            if c < 3:
+                raw, lo = wu_raw, c * CH
             else:
                 raw, lo = wv_raw, (c - 3) * CH
             return raw[:, 2 * g : 2 * g + 2, :, lo : lo + CH].rearrange("p u e n -> p (u e) n")
@@ -123,15 +125,15 @@ def tile_gatedattentionunit_pa_kernel(
 
         xg = {}
 
-        def x_transpose(i):
+        def x_transpose(i, copy):
             d, r = divmod(i, 2)
             if r == 0:
                 xg[d] = xgp.tile([P, 2, 2, P, 4], BF16, name="xg%d" % d, tag="xg", align_bytes=64)
             xt = psum.tile([P, 4, P], F32, name="xt%d" % i, tag="bank")
-            words = x_raw[d][:, r, :].bitcast(F32)
+            words = x_raw[i // 4][:, i % 4, :].bitcast(F32)
             for b in range(4):
                 nc.tensor.transpose(xt[:, b, :], words[:, b * P : (b + 1) * P], ident[:])
-            nc.scalar.copy(
+            copy(
                 out=xg[d][:, r, :, :, :].bitcast(F32),
                 in_=xt[:].rearrange("p (g u) r -> p g r u", u=2),
             )
@@ -166,74 +168,63 @@ def tile_gatedattentionunit_pa_kernel(
             return stage.tile([P, 2, E], F32, name=name, tag="stage")
 
         regroup((0, 0))
-        regroup((0, 1))
+        regroup((1, 0))
         quantise((0, 0))
-        x_transpose(0)
-        x_transpose(1)
+        regroup((2, 0))
+        quantise((1, 0))
+        quantise((2, 0))
+        for i in range(4):
+            x_transpose(i, nc.scalar.copy)
         x_quantise(0)
+        x_quantise(1)
+        regroup((0, 1))
+        regroup((1, 1))
         quantise((0, 1))
-        for d in range(1, 4):
-            x_transpose(2 * d)
-            x_transpose(2 * d + 1)
-            x_quantise(d)
+        regroup((2, 1))
+        quantise((1, 1))
+        quantise((2, 1))
+        x_transpose(4, nc.scalar.copy)
+        x_transpose(5, nc.scalar.copy)
+        x_quantise(2)
+
+        def store_pair(dram, j, pair):
+            nc.sync.dma_start(out=dram[j, :, :, :], in_=pair[:])
 
         u_sb = [pair_tile("u_sb%d" % j) for j in range(NT // 2)]
-        for i in range(NT):
+        for i in range(4):
             mx_chunk(i, 0, u_sb[i // 2])
-        regroup((1, 0))
-        regroup((2, 0))
-        regroup((1, 1))
-        quantise((1, 0))
-        quantise((1, 1))
-        regroup((2, 1))
-        quantise((2, 0))
-        quantise((2, 1))
-        for i in range(4):
-            mx_chunk(i, 1, u_sb[i // 2])
-        for i in range(4):
-            mx_chunk(i, 2, u_sb[i // 2])
-            if i % 2 == 1:
-                nc.sync.dma_start(out=u_dram[i // 2, :, :, :], in_=u_sb[i // 2][:])
-        for i in range(4, NT):
-            mx_chunk(i, 1, u_sb[i // 2])
-            mx_chunk(i, 2, u_sb[i // 2])
-            if i % 2 == 1:
-                nc.sync.dma_start(out=u_dram[i // 2, :, :, :], in_=u_sb[i // 2][:])
-
+        for c in (1, 2):
+            for i in (0, 1):
+                mx_chunk(i, c, u_sb[0])
+        store_pair(u_dram, 0, u_sb[0])
         regroup((3, 0))
         regroup((4, 0))
         quantise((3, 0))
-        regroup((3, 1))
-        quantise((4, 0))
-        regroup("qk")
-        quantise((3, 1))
-        regroup((4, 1))
-        quantise("qk")
+        x_transpose(6, nc.vector.tensor_copy)
+        x_transpose(7, nc.vector.tensor_copy)
+        for i in (2, 3):
+            for c in (1, 2):
+                mx_chunk(i, c, u_sb[1])
+        store_pair(u_dram, 1, u_sb[1])
+
         regroup((5, 0))
-        quantise((4, 1))
-        regroup((5, 1))
+        quantise((4, 0))
+        x_quantise(3)
+        regroup("qk")
         quantise((5, 0))
+        regroup((3, 1))
+        quantise("qk")
+        regroup((4, 1))
+        quantise((3, 1))
+        regroup((5, 1))
+        quantise((4, 1))
         quantise((5, 1))
 
-        v_sb = [pair_tile("v_sb%d" % j) for j in range(2)]
-        for i in range(4):
-            mx_chunk(i, 3, v_sb[i // 2])
-
-        gps = psum.tile([P, CH], F32, name="gps", tag="bank")
-        nc.tensor.matmul(out=gps[:, 0 : 2 * D], lhsT=ones[:], rhs=gsrc[:], start=True, stop=True)
-        nc.scalar.copy(out=gains[:].rearrange("p s d -> p (s d)"), in_=gps[:, 0 : 2 * D])
-        for h in range(2):
-            zb = psum.tile([P, 4, D], F32, name="zb%d" % h, tag="bank")
-            for r in range(4):
-                mx(zb[:, r, :], 4 * h + r, lambda g: wq_codes[:, g, :], lambda g: wq_scales[:, g, :])
-            nc.scalar.activation(out=z[:, 4 * h : 4 * h + 4, :], in_=zb[:], func=SILU)
-
-        for i in range(4):
-            mx_chunk(i, 4, v_sb[i // 2])
-        for i in range(4):
-            mx_chunk(i, 5, v_sb[i // 2])
-            if i % 2 == 1:
-                nc.sync.dma_start(out=v_dram[i // 2, :, :, :], in_=v_sb[i // 2][:])
+        for j in (2, 3):
+            for i in (2 * j, 2 * j + 1):
+                for c in range(3):
+                    mx_chunk(i, c, u_sb[j])
+            store_pair(u_dram, j, u_sb[j])
 
         def rotate(s, dram):
             y = rot.tile([P, NT, D], F32, name="y%d" % s, tag="y")
@@ -254,17 +245,37 @@ def tile_gatedattentionunit_pa_kernel(
             nc.vector.tensor_tensor(out=m_cos[:, :, 1, :], in0=m_cos[:, :, 1, :], in1=m_sin[:, :, 0, :], op=ADD)
             nc.sync.dma_start(out=dram, in_=m_cos[:].rearrange("p i h j -> p i (h j)"))
 
-        rotate(0, q_dram)
-        v45 = pair_tile("v_sb2")
-        for i in (4, 5):
+        def v_tile(i, pair):
             for c in range(3, 6):
-                mx_chunk(i, c, v45)
-        nc.sync.dma_start(out=v_dram[2, :, :, :], in_=v45[:])
-        v67 = pair_tile("v_sb3")
-        for c in range(3, 6):
-            mx_chunk(6, c, v67)
-        nc.sync.dma_start(out=v_dram[3, :, 0, :], in_=v67[:, 0, :])
+                mx_chunk(i, c, pair)
+
+        gps = psum.tile([P, CH], F32, name="gps", tag="bank")
+        nc.tensor.matmul(out=gps[:, 0 : 2 * D], lhsT=ones[:], rhs=gsrc[:], start=True, stop=True)
+        nc.scalar.copy(out=gains[:].rearrange("p s d -> p (s d)"), in_=gps[:, 0 : 2 * D])
+        for h in range(2):
+            zb = psum.tile([P, 4, D], F32, name="zb%d" % h, tag="bank")
+            for r in range(4):
+                mx(zb[:, r, :], 4 * h + r, lambda g: wq_codes[:, g, :], lambda g: wq_scales[:, g, :])
+            nc.scalar.activation(out=z[:, 4 * h : 4 * h + 4, :], in_=zb[:], func=SILU)
+
+        v01 = pair_tile("v_sb0")
+        v_tile(0, v01)
+        v_tile(1, v01)
+        store_pair(v_dram, 0, v01)
+        rotate(0, q_dram)
+
+        v23 = pair_tile("v_sb1")
+        v_tile(2, v23)
+        v_tile(3, v23)
+        store_pair(v_dram, 1, v23)
+
+        v45 = pair_tile("v_sb2")
+        v_tile(4, v45)
+        v_tile(5, v45)
+        store_pair(v_dram, 2, v45)
         rotate(1, k_dram)
-        for c in range(3, 6):
-            mx_chunk(7, c, v67)
+        v67 = pair_tile("v_sb3")
+        v_tile(6, v67)
+        nc.sync.dma_start(out=v_dram[3, :, 0, :], in_=v67[:, 0, :])
+        v_tile(7, v67)
         nc.sync.dma_start(out=v_dram[3, :, 1, :], in_=v67[:, 1, :])

@@ -30,6 +30,7 @@ def tile_gatedattentionunit_pa_kernel(
     x_dram = hidden_states.flatten_outer_dims().rearrange("(p i) k -> p i k", i=NT)
     cos_dram = cos.flatten_outer_dims().rearrange("(p i) j -> p i j", i=NT)
     sin_dram = sin.flatten_outer_dims().rearrange("(p i) j -> p i j", i=NT)
+    w_by_e = W_i.rearrange("(a q e) n -> e q a n", a=4, e=2)
     w_by_a = W_i.rearrange("(a q e) n -> a q e n", a=4, e=2)
     u_dram = out_0.flatten_outer_dims().rearrange("(p j r) c -> j p r c", j=NT // 2, r=2)
     v_dram = out_1.flatten_outer_dims().rearrange("(p j r) c -> j p r c", j=NT // 2, r=2)
@@ -57,27 +58,24 @@ def tile_gatedattentionunit_pa_kernel(
         wq_codes = keep.tile([P, 2, D], U32, name="wq_codes", align_bytes=64)
         wq_scales = keep.tile([P, 2, D], U8, name="wq_scales", align_bytes=64)
         wq_grp = keep.tile([P, 2, D, 4], BF16, name="wq_grp", align_bytes=64)
-        wu_raw = keep.tile([P, 4, 2, E], BF16, name="wu_raw")
+        w0_raw = keep.tile([P, 4, 2, CH], BF16, name="w0_raw")
+        w12_raw = keep.tile([P, 4, 2, 2 * CH], BF16, name="w12_raw")
         wv_raw = keep.tile([P, 4, 2, VW], BF16, name="wv_raw")
         z = keep.tile([P, NT, D], F32, name="z")
-        x_raw = [keep.tile([P, 4, 1024], BF16, name="x_raw%d" % h) for h in range(2)]
+        x_raw = [keep.tile([P, 2, 1024], BF16, name="x_raw%d" % d) for d in range(4)]
 
         make_identity(nc, ident[:])
         nc.gpsimd.memset(ones[:], 1.0)
         nc.gpsimd.memset(gsrc[:], 0.0)
 
-        def load_wu(a):
-            nc.sync.dma_start(out=wu_raw[:, a, :, :], in_=w_by_a[a, :, :, 0:E])
-
-        def load_x(h):
-            nc.sync.dma_start(out=x_raw[h][:], in_=x_dram[:, 4 * h : 4 * h + 4, :])
-
-        load_wu(0)
-        load_wu(1)
-        load_x(0)
-        load_wu(2)
-        load_wu(3)
-        load_x(1)
+        for e in range(2):
+            nc.sync.dma_start(out=w0_raw[:, :, e, :], in_=w_by_e[e, :, :, 0:CH])
+        for d in range(2):
+            nc.sync.dma_start(out=x_raw[d][:], in_=x_dram[:, 2 * d : 2 * d + 2, :])
+        for a in range(4):
+            nc.sync.dma_start(out=w12_raw[:, a, :, :], in_=w_by_a[a, :, :, CH:E])
+        for d in range(2, 4):
+            nc.sync.dma_start(out=x_raw[d][:], in_=x_dram[:, 2 * d : 2 * d + 2, :])
         for a in range(4):
             nc.sync.dma_start(out=wv_raw[:, a, :, :], in_=w_by_a[a, :, :, E : E + VW])
         nc.sync.dma_start(out=tab[:, 0, :, :], in_=cos_dram)
@@ -86,8 +84,10 @@ def tile_gatedattentionunit_pa_kernel(
         nc.sync.dma_start(out=gsrc[0:1, D : 2 * D], in_=k_scale.rearrange("(o d) -> o d", o=1))
 
         def w_src(c, g):
-            if c < 3:
-                raw, lo = wu_raw, c * CH
+            if c == 0:
+                raw, lo = w0_raw, 0
+            elif c < 3:
+                raw, lo = w12_raw, (c - 1) * CH
             else:
                 raw, lo = wv_raw, (c - 3) * CH
             return raw[:, 2 * g : 2 * g + 2, :, lo : lo + CH].rearrange("p u e n -> p (u e) n")
@@ -125,15 +125,15 @@ def tile_gatedattentionunit_pa_kernel(
 
         xg = {}
 
-        def x_transpose(i, copy):
+        def x_transpose(i):
             d, r = divmod(i, 2)
             if r == 0:
                 xg[d] = xgp.tile([P, 2, 2, P, 4], BF16, name="xg%d" % d, tag="xg", align_bytes=64)
             xt = psum.tile([P, 4, P], F32, name="xt%d" % i, tag="bank")
-            words = x_raw[i // 4][:, i % 4, :].bitcast(F32)
+            words = x_raw[d][:, r, :].bitcast(F32)
             for b in range(4):
                 nc.tensor.transpose(xt[:, b, :], words[:, b * P : (b + 1) * P], ident[:])
-            copy(
+            nc.scalar.copy(
                 out=xg[d][:, r, :, :, :].bitcast(F32),
                 in_=xt[:].rearrange("p (g u) r -> p g r u", u=2),
             )
@@ -168,24 +168,15 @@ def tile_gatedattentionunit_pa_kernel(
             return stage.tile([P, 2, E], F32, name=name, tag="stage")
 
         regroup((0, 0))
-        regroup((1, 0))
-        quantise((0, 0))
-        regroup((2, 0))
-        quantise((1, 0))
-        quantise((2, 0))
-        for i in range(4):
-            x_transpose(i, nc.scalar.copy)
-        x_quantise(0)
-        x_quantise(1)
         regroup((0, 1))
-        regroup((1, 1))
+        quantise((0, 0))
+        x_transpose(0)
+        x_transpose(1)
+        x_quantise(0)
         quantise((0, 1))
-        regroup((2, 1))
-        quantise((1, 1))
-        quantise((2, 1))
-        x_transpose(4, nc.scalar.copy)
-        x_transpose(5, nc.scalar.copy)
-        x_quantise(2)
+        x_transpose(2)
+        x_transpose(3)
+        x_quantise(1)
 
         def store_pair(dram, j, pair):
             nc.sync.dma_start(out=dram[j, :, :, :], in_=pair[:])
@@ -193,23 +184,32 @@ def tile_gatedattentionunit_pa_kernel(
         u_sb = [pair_tile("u_sb%d" % j) for j in range(NT // 2)]
         for i in range(4):
             mx_chunk(i, 0, u_sb[i // 2])
-        for c in (1, 2):
-            for i in (0, 1):
-                mx_chunk(i, c, u_sb[0])
-        store_pair(u_dram, 0, u_sb[0])
+        regroup((1, 0))
+        regroup((2, 0))
+        regroup((1, 1))
+        quantise((1, 0))
+        quantise((1, 1))
+        regroup((2, 1))
+        quantise((2, 0))
+        quantise((2, 1))
+        x_transpose(4)
+        x_transpose(5)
+        x_quantise(2)
+        for i in range(4):
+            mx_chunk(i, 1, u_sb[i // 2])
+        for i in range(4):
+            mx_chunk(i, 2, u_sb[i // 2])
+            if i % 2 == 1:
+                store_pair(u_dram, i // 2, u_sb[i // 2])
+        x_transpose(6)
+        x_transpose(7)
+
         regroup((3, 0))
         regroup((4, 0))
         quantise((3, 0))
-        x_transpose(6, nc.vector.tensor_copy)
-        x_transpose(7, nc.vector.tensor_copy)
-        for i in (2, 3):
-            for c in (1, 2):
-                mx_chunk(i, c, u_sb[1])
-        store_pair(u_dram, 1, u_sb[1])
-
+        x_quantise(3)
         regroup((5, 0))
         quantise((4, 0))
-        x_quantise(3)
         regroup("qk")
         quantise((5, 0))
         regroup((3, 1))
@@ -225,6 +225,15 @@ def tile_gatedattentionunit_pa_kernel(
                 for c in range(3):
                     mx_chunk(i, c, u_sb[j])
             store_pair(u_dram, j, u_sb[j])
+
+        gps = psum.tile([P, CH], F32, name="gps", tag="bank")
+        nc.tensor.matmul(out=gps[:, 0 : 2 * D], lhsT=ones[:], rhs=gsrc[:], start=True, stop=True)
+        nc.scalar.copy(out=gains[:].rearrange("p s d -> p (s d)"), in_=gps[:, 0 : 2 * D])
+        for h in range(2):
+            zb = psum.tile([P, 4, D], F32, name="zb%d" % h, tag="bank")
+            for r in range(4):
+                mx(zb[:, r, :], 4 * h + r, lambda g: wq_codes[:, g, :], lambda g: wq_scales[:, g, :])
+            nc.scalar.activation(out=z[:, 4 * h : 4 * h + 4, :], in_=zb[:], func=SILU)
 
         def rotate(s, dram):
             y = rot.tile([P, NT, D], F32, name="y%d" % s, tag="y")
@@ -249,26 +258,15 @@ def tile_gatedattentionunit_pa_kernel(
             for c in range(3, 6):
                 mx_chunk(i, c, pair)
 
-        gps = psum.tile([P, CH], F32, name="gps", tag="bank")
-        nc.tensor.matmul(out=gps[:, 0 : 2 * D], lhsT=ones[:], rhs=gsrc[:], start=True, stop=True)
-        nc.scalar.copy(out=gains[:].rearrange("p s d -> p (s d)"), in_=gps[:, 0 : 2 * D])
-        for h in range(2):
-            zb = psum.tile([P, 4, D], F32, name="zb%d" % h, tag="bank")
-            for r in range(4):
-                mx(zb[:, r, :], 4 * h + r, lambda g: wq_codes[:, g, :], lambda g: wq_scales[:, g, :])
-            nc.scalar.activation(out=z[:, 4 * h : 4 * h + 4, :], in_=zb[:], func=SILU)
-
         v01 = pair_tile("v_sb0")
         v_tile(0, v01)
         v_tile(1, v01)
         store_pair(v_dram, 0, v01)
         rotate(0, q_dram)
-
         v23 = pair_tile("v_sb1")
         v_tile(2, v23)
         v_tile(3, v23)
         store_pair(v_dram, 1, v23)
-
         v45 = pair_tile("v_sb2")
         v_tile(4, v45)
         v_tile(5, v45)

from contextlib import ExitStack

import concourse.mybir as mybir
from concourse.masks import make_identity

F32 = mybir.dt.float32
BF16 = mybir.dt.bfloat16
U32 = mybir.dt.uint32
U8 = mybir.dt.uint8
FP8X4 = mybir.dt.float8_e4m3fn_x4
SILU = mybir.ActivationFunctionType.Silu
MULT = mybir.AluOpType.mult
ADD = mybir.AluOpType.add
SUB = mybir.AluOpType.subtract

P = 128
NT = 8
E = 1536
D = 128
CH = 512
VW = E + D

FLOPS = 2 * 1024 * 1024 * 3200


def tile_gatedattentionunit_pa_kernel(
    tc, hidden_states, sin, cos, W_i, q_scale, k_scale, out_0, out_1, out_2, out_3
):
    nc = tc.nc
    x_dram = hidden_states.flatten_outer_dims().rearrange("(p i) k -> p i k", i=NT)
    cos_dram = cos.flatten_outer_dims().rearrange("(p i) j -> p i j", i=NT)
    sin_dram = sin.flatten_outer_dims().rearrange("(p i) j -> p i j", i=NT)
    w_by_e = W_i.rearrange("(a q e) n -> e q a n", a=4, e=2)
    w_by_a = W_i.rearrange("(a q e) n -> a q e n", a=4, e=2)
    u_dram = out_0.flatten_outer_dims().rearrange("(p j r) c -> j p r c", j=NT // 2, r=2)
    v_dram = out_1.flatten_outer_dims().rearrange("(p j r) c -> j p r c", j=NT // 2, r=2)
    q_dram = out_2.flatten_outer_dims().rearrange("(p i) c -> p i c", i=NT)
    k_dram = out_3.flatten_outer_dims().rearrange("(p i) c -> p i c", i=NT)

    with ExitStack() as ctx:
        keep = ctx.enter_context(tc.tile_pool(name="keep", bufs=1))
        xgp = ctx.enter_context(tc.tile_pool(name="xgp", bufs=3))
        wgp = ctx.enter_context(tc.tile_pool(name="wgp", bufs=3))
        stage = ctx.enter_context(tc.tile_pool(name="stage", bufs=6))
        rot = ctx.enter_context(tc.tile_pool(name="rot", bufs=1))
        psum = ctx.enter_context(tc.psum_pool(name="psum", bufs=8))
        ctx.enter_context(tc.manual_schedule())

        ident = keep.tile([P, P], F32, name="ident")
        ones = keep.tile([P, P], BF16, name="ones")
        gsrc = keep.tile([P, 2 * D], BF16, name="gsrc")
        gains = keep.tile([P, 2, D], F32, name="gains")
        tab = keep.tile([P, 2, NT, D // 2], BF16, name="tab")
        x_codes = keep.tile([P, NT, 2, P], U32, name="x_codes", align_bytes=64)
        x_scales = keep.tile([P, NT, 2, P], U8, name="x_scales", align_bytes=64)
        w_codes = keep.tile([P, 2, 2 * E], U32, name="w_codes", align_bytes=64)
        w_scales = keep.tile([P, 2, 2 * E], U8, name="w_scales", align_bytes=64)
        wq_codes = keep.tile([P, 2, D], U32, name="wq_codes", align_bytes=64)
        wq_scales = keep.tile([P, 2, D], U8, name="wq_scales", align_bytes=64)
        wq_grp = keep.tile([P, 2, D, 4], BF16, name="wq_grp", align_bytes=64)
        w0_raw = keep.tile([P, 4, 2, CH], BF16, name="w0_raw")
        w12_raw = keep.tile([P, 4, 2, 2 * CH], BF16, name="w12_raw")
        wv_raw = keep.tile([P, 4, 2, VW], BF16, name="wv_raw")
        z = keep.tile([P, NT, D], F32, name="z")
        x_raw = [keep.tile([P, 2, 1024], BF16, name="x_raw%d" % d) for d in range(4)]

        make_identity(nc, ident[:])
        nc.gpsimd.memset(ones[:], 1.0)
        nc.gpsimd.memset(gsrc[:], 0.0)

        for e in range(2):
            nc.sync.dma_start(out=w0_raw[:, :, e, :], in_=w_by_e[e, :, :, 0:CH])
        for d in range(2):
            nc.sync.dma_start(out=x_raw[d][:], in_=x_dram[:, 2 * d : 2 * d + 2, :])
        for a in range(4):
            nc.sync.dma_start(out=w12_raw[:, a, :, :], in_=w_by_a[a, :, :, CH:E])
        for d in range(2, 4):
            nc.sync.dma_start(out=x_raw[d][:], in_=x_dram[:, 2 * d : 2 * d + 2, :])
        for a in range(4):
            nc.sync.dma_start(out=wv_raw[:, a, :, :], in_=w_by_a[a, :, :, E : E + VW])
        nc.sync.dma_start(out=tab[:, 0, :, :], in_=cos_dram)
        nc.sync.dma_start(out=tab[:, 1, :, :], in_=sin_dram)
        nc.sync.dma_start(out=gsrc[0:1, 0:D], in_=q_scale.rearrange("(o d) -> o d", o=1))
        nc.sync.dma_start(out=gsrc[0:1, D : 2 * D], in_=k_scale.rearrange("(o d) -> o d", o=1))

        def w_src(c, g):
            if c == 0:
                raw, lo = w0_raw, 0
            elif c < 3:
                raw, lo = w12_raw, (c - 1) * CH
            else:
                raw, lo = wv_raw, (c - 3) * CH
            return raw[:, 2 * g : 2 * g + 2, :, lo : lo + CH].rearrange("p u e n -> p (u e) n")

        grouped = {}

        def regroup(job):
            if job == "qk":
                src = wv_raw[:, :, :, E : E + D].rearrange("p (g u) e n -> p g (u e) n", g=2)
                nc.vector.tensor_copy(out=wq_grp[:], in_=src.rearrange("p g t n -> p g n t"))
                return
            c, g = job
            t = wgp.tile([P, CH, 4], BF16, name="wgrp%d_%d" % (c, g), tag="wgrp", align_bytes=64)
            nc.vector.tensor_copy(
                out=t[:].rearrange("p (n i) t -> p n t i", i=4),
                in_=w_src(c, g).rearrange("p t (n i) -> p n t i", i=4),
            )
            grouped[job] = t

        def quantise(job):
            if job == "qk":
                nc.vector.quantize_mx(
                    out=wq_codes[:].rearrange("p g n -> p (g n)").bitcast(FP8X4),
                    scales=wq_scales[:].rearrange("p g n -> p (g n)"),
                    in_=wq_grp[:].rearrange("p g n t -> p (g n t)"),
                )
                return
            c, g = job
            cols = slice(c * CH, (c + 1) * CH)
            nc.vector.quantize_mx(
                out=w_codes[:, g, cols].bitcast(FP8X4),
                scales=w_scales[:, g, cols],
                in_=grouped[job][:].rearrange("p n t -> p (n t)"),
            )

        xg = {}

        def x_transpose(i):
            d, r = divmod(i, 2)
            if r == 0:
                xg[d] = xgp.tile([P, 2, 2, P, 4], BF16, name="xg%d" % d, tag="xg", align_bytes=64)
            xt = psum.tile([P, 4, P], F32, name="xt%d" % i, tag="bank")
            words = x_raw[d][:, r, :].bitcast(F32)
            for b in range(4):
                nc.tensor.transpose(xt[:, b, :], words[:, b * P : (b + 1) * P], ident[:])
            nc.scalar.copy(
                out=xg[d][:, r, :, :, :].bitcast(F32),
                in_=xt[:].rearrange("p (g u) r -> p g r u", u=2),
            )

        def x_quantise(d):
            nc.vector.quantize_mx(
                out=x_codes[:, 2 * d : 2 * d + 2].rearrange("p i g r -> p (i g r)").bitcast(FP8X4),
                scales=x_scales[:, 2 * d : 2 * d + 2].rearrange("p i g r -> p (i g r)"),
                in_=xg[d][:].rearrange("p i g r t -> p (i g r t)"),
            )

        def mx(acc, i, codes, scales):
            for g in range(2):
                nc.tensor.matmul_mx(
                    out=acc,
                    lhsT=x_codes[:, i, g, :].bitcast(FP8X4),
                    lhsT_scale=x_scales[:, i, g, :],
                    rhs=codes(g).bitcast(FP8X4),
                    rhs_scale=scales(g),
                    start=(g == 0),
                    stop=(g == 1),
                )

        def mx_chunk(i, c, pair):
            cols = slice(c * CH, (c + 1) * CH)
            acc = psum.tile([P, CH], F32, name="acc%d_%d" % (c, i), tag="bank")
            mx(acc[:], i, lambda g: w_codes[:, g, cols], lambda g: w_scales[:, g, cols])
            lo = (c % 3) * CH
            nc.scalar.activation(out=pair[:, i % 2, lo : lo + CH], in_=acc[:], func=SILU)

        def pair_tile(name):
            return stage.tile([P, 2, E], F32, name=name, tag="stage")

        regroup((0, 0))
        regroup((0, 1))
        quantise((0, 0))
        x_transpose(0)
        x_transpose(1)
        x_quantise(0)
        quantise((0, 1))
        x_transpose(2)
        x_transpose(3)
        x_quantise(1)

        def store_pair(dram, j, pair):
            nc.sync.dma_start(out=dram[j, :, :, :], in_=pair[:])

        u_sb = [pair_tile("u_sb%d" % j) for j in range(NT // 2)]
        for i in range(4):
            mx_chunk(i, 0, u_sb[i // 2])
        regroup((1, 0))
        regroup((2, 0))
        regroup((1, 1))
        quantise((1, 0))
        quantise((1, 1))
        regroup((2, 1))
        quantise((2, 0))
        quantise((2, 1))
        x_transpose(4)
        x_transpose(5)
        x_quantise(2)
        for i in range(4):
            mx_chunk(i, 1, u_sb[i // 2])
        for i in range(4):
            mx_chunk(i, 2, u_sb[i // 2])
            if i % 2 == 1:
                store_pair(u_dram, i // 2, u_sb[i // 2])
        x_transpose(6)
        x_transpose(7)

        regroup((3, 0))
        regroup((4, 0))
        quantise((3, 0))
        x_quantise(3)
        regroup((5, 0))
        quantise((4, 0))
        regroup("qk")
        quantise((5, 0))
        regroup((3, 1))
        quantise("qk")
        regroup((4, 1))
        quantise((3, 1))
        regroup((5, 1))
        quantise((4, 1))
        quantise((5, 1))

        for j in (2, 3):
            for i in (2 * j, 2 * j + 1):
                for c in range(3):
                    mx_chunk(i, c, u_sb[j])
            store_pair(u_dram, j, u_sb[j])

        gps = psum.tile([P, CH], F32, name="gps", tag="bank")
        nc.tensor.matmul(out=gps[:, 0 : 2 * D], lhsT=ones[:], rhs=gsrc[:], start=True, stop=True)
        nc.scalar.copy(out=gains[:].rearrange("p s d -> p (s d)"), in_=gps[:, 0 : 2 * D])
        for h in range(2):
            zb = psum.tile([P, 4, D], F32, name="zb%d" % h, tag="bank")
            for r in range(4):
                mx(zb[:, r, :], 4 * h + r, lambda g: wq_codes[:, g, :], lambda g: wq_scales[:, g, :])
            nc.scalar.activation(out=z[:, 4 * h : 4 * h + 4, :], in_=zb[:], func=SILU)

        def rotate(s, dram):
            y = rot.tile([P, NT, D], F32, name="y%d" % s, tag="y")
            m_cos = rot.tile([P, NT, 2, D // 2], F32, name="mc%d" % s, tag="mc", bufs=2)
            m_sin = rot.tile([P, NT, 2, D // 2], F32, name="ms%d" % s, tag="ms")
            nc.vector.tensor_tensor(
                out=y[:], in0=z[:], in1=gains[:, s, :].unsqueeze(1).to_broadcast([P, NT, D]), op=MULT
            )
            pairs = y[:].rearrange("p i (j e) -> p i e j", e=2)
            shape = [P, NT, 2, D // 2]
            nc.vector.tensor_tensor(
                out=m_cos[:], in0=pairs, in1=tab[:, 0, :, :].unsqueeze(2).to_broadcast(shape), op=MULT
            )
            nc.vector.tensor_tensor(
                out=m_sin[:], in0=pairs, in1=tab[:, 1, :, :].unsqueeze(2).to_broadcast(shape), op=MULT
            )
            nc.vector.tensor_tensor(out=m_cos[:, :, 0, :], in0=m_cos[:, :, 0, :], in1=m_sin[:, :, 1, :], op=SUB)
            nc.vector.tensor_tensor(out=m_cos[:, :, 1, :], in0=m_cos[:, :, 1, :], in1=m_sin[:, :, 0, :], op=ADD)
            nc.sync.dma_start(out=dram, in_=m_cos[:].rearrange("p i h j -> p i (h j)"))

        def v_tile(i, pair):
            for c in range(3, 6):
                mx_chunk(i, c, pair)

        v01 = pair_tile("v_sb0")
        v_tile(0, v01)
        v_tile(1, v01)
        store_pair(v_dram, 0, v01)
        rotate(0, q_dram)
        v23 = pair_tile("v_sb1")
        v_tile(2, v23)
        v_tile(3, v23)
        store_pair(v_dram, 1, v23)
        v45 = pair_tile("v_sb2")
        v_tile(4, v45)
        v_tile(5, v45)
        store_pair(v_dram, 2, v45)
        rotate(1, k_dram)
        v67 = pair_tile("v_sb3")
        v_tile(6, v67)
        nc.sync.dma_start(out=v_dram[3, :, 0, :], in_=v67[:, 0, :])
        v_tile(7, v67)
        nc.sync.dma_start(out=v_dram[3, :, 1, :], in_=v67[:, 1, :])
